import numpy as np
import ml_dtypes


def mxq(x, axis, fmt="e4m3"):
    dtype, down = {"e4m3": (ml_dtypes.float8_e4m3fn, 7), "e5m2": (ml_dtypes.float8_e5m2, 14)}[fmt]
    v = np.moveaxis(np.asarray(x, np.float32).astype(ml_dtypes.bfloat16).astype(np.float64), axis, -1)
    blocks = v.reshape(v.shape[:-1] + (-1, 32))
    amax = np.abs(blocks).max(-1, keepdims=True)
    byte = np.maximum(np.where(amax > 0, np.frexp(amax)[1] - 1 + 127, 0) - down, 1)
    scale = np.exp2(byte - 127.0)
    codes = (blocks / scale).astype(np.float32).astype(dtype).astype(np.float64)
    return np.moveaxis((codes * scale).reshape(v.shape), -1, axis)


WIDE = False


def mx_kscale(k):
    if not WIDE:
        return np.ones(k)
    levels = np.array([20, -20, 10, -10, 0])
    a = np.random.permutation(np.resize(levels, k // 512 * 4)).reshape(k // 512, 4)
    idx = np.arange(k)
    return np.exp2(a[idx // 512, idx % 128 // 32])


BF16 = ml_dtypes.bfloat16


def bf(x):
    return np.asarray(x, np.float32).astype(BF16)


def f64(x):
    return np.asarray(x).astype(np.float64)


B, T, D, F = 2, 512, 512, 512
BINS = np.array([-1.5, -1.0, -0.5, 0.0, 0.5, 1.0, 1.5])
NB = BINS.shape[0] + 1
INDEX = 0


def buckets(x):
    y = x[..., INDEX]
    return np.sum(np.where(y[..., None] > BINS, 1.0, 0.0), axis=-1).reshape(B * T)


def setup_inputs():
    u = mx_kscale(F)
    x = np.random.standard_normal((B, T, D))
    W = np.random.standard_normal((NB, D, F)) * 0.5 / np.sqrt(D) / u[None, None, :]
    g = np.random.standard_normal((B, T, F)) * np.exp2(np.random.randint(-12, 1, (B, T, 1))) * 16.0 * u
    y = x[..., INDEX]
    near = np.min(np.abs(y[..., None] - BINS), axis=-1) < 0.01
    x[..., INDEX] = np.where(near, y + 0.03, y)
    return {"x": bf(x), "W": bf(W), "grad_out": bf(g)}


def reference(x, W, grad_out):
    x, W, g = f64(x), f64(W), f64(grad_out)
    memf = buckets(x)
    gq = mxq(g.reshape(B * T, F), 1, "e5m2")
    Wq = mxq(W, 2, "e4m3")
    out = np.zeros((B * T, D))
    for k in range(NB):
        sel = np.where(memf == k, 1.0, 0.0)[:, None]
        out = out + sel * (gq @ Wq[k].T)
    return out.reshape(B, T, D)

@@ -1,0 +1,171 @@
+from contextlib import ExitStack
+
+import concourse.masks as masks
+import concourse.mybir as mybir
+
+F32 = mybir.dt.float32
+BF16 = mybir.dt.bfloat16
+U32 = mybir.dt.uint32
+U8 = mybir.dt.uint8
+E4M3X4 = mybir.dt.float8_e4m3fn_x4
+E5M2X4 = mybir.dt.float8_e5m2_x4
+ALU = mybir.AluOpType
+COPY = mybir.ActivationFunctionType.Copy
+
+P = 128
+TOKENS = 1024
+D = 512
+F = 512
+BOUNDS = (-1.5, -1.0, -0.5, 0.0, 0.5, 1.0, 1.5)
+EXPERTS = len(BOUNDS) + 1
+HALVES = 2
+ROUNDS = EXPERTS // HALVES
+TOKEN_TILES = TOKENS // P
+ROW_TILES = D // P
+PACK = 4
+WORD_HALVES = 2
+BANK_WORDS = 512
+X_RUN = 16
+
+FLOPS = 2 * EXPERTS * TOKENS * D * F
+BYTES = 2 * EXPERTS * D * F + 2 * TOKENS * F + 4 * TOKENS * D + 2 * TOKENS
+
+
+def tile_dispatchbyvariable_pa_kernel(tc, x, W, grad_out, out):
+    nc = tc.nc
+    x_rows = x.flatten_outer_dims().rearrange("(i p) d -> p i d", p=P)
+    g_rows = grad_out.flatten_outer_dims().rearrange("(i p) f -> p i f", p=P)
+    out_rows = out.flatten_outer_dims().rearrange("(i p) d -> p i d", p=P)
+    w_rows = W.rearrange("k (r p) f -> p k r f", p=P)
+
+    first_tiles = range(0, TOKEN_TILES // 2)
+    last_tiles = range(TOKEN_TILES // 2, TOKEN_TILES)
+
+    with ExitStack() as ctx:
+        keep = ctx.enter_context(tc.tile_pool(name="keep", bufs=1))
+        words_psum = ctx.enter_context(tc.psum_pool(name="words_psum", bufs=4))
+        product_psum = ctx.enter_context(tc.psum_pool(name="product_psum", bufs=4))
+        ctx.enter_context(tc.manual_schedule())
+
+        y_raw = keep.tile([P, TOKEN_TILES, X_RUN], BF16)
+        g_raw = [keep.tile([P, TOKEN_TILES // 2, F], BF16, name="g_raw%d" % c) for c in range(2)]
+        w_raw = [keep.tile([P, ROW_TILES, F], BF16, name="w_raw%d" % k) for k in range(EXPERTS)]
+        g_grouped = [
+            keep.tile([P, HALVES * P * PACK], BF16, name="g_grouped%d" % i, align_bytes=64)
+            for i in range(TOKEN_TILES)
+        ]
+        g_codes = [
+            keep.tile([P, HALVES * P], U32, name="g_codes%d" % i, align_bytes=64) for i in range(TOKEN_TILES)
+        ]
+        g_scales = [
+            keep.tile([P, HALVES * P], U8, name="g_scales%d" % i, align_bytes=64) for i in range(TOKEN_TILES)
+        ]
+        w_grouped = [keep.tile([P, D * PACK], BF16, name="w_grouped%d" % k, align_bytes=64) for k in range(EXPERTS)]
+        w_codes = [keep.tile([P, D], U32, name="w_codes%d" % k, align_bytes=64) for k in range(EXPERTS)]
+        w_scales = [keep.tile([P, D], U8, name="w_scales%d" % k, align_bytes=64) for k in range(EXPERTS)]
+        acc = [keep.tile([P, D], F32, name="acc%d" % i) for i in range(TOKEN_TILES)]
+
+        nc.sync.dma_start(out=y_raw[:], in_=x_rows[:, :, 0:X_RUN])
+        nc.sync.dma_start(out=w_raw[0][:], in_=w_rows[:, 0])
+        nc.sync.dma_start(out=w_raw[ROUNDS][:], in_=w_rows[:, ROUNDS])
+        nc.sync.dma_start(out=g_raw[0][:], in_=g_rows[:, 0 : TOKEN_TILES // 2, :])
+        nc.sync.dma_start(out=g_raw[1][:], in_=g_rows[:, TOKEN_TILES // 2 : TOKEN_TILES, :])
+        for j in range(1, ROUNDS):
+            nc.sync.dma_start(out=w_raw[j][:], in_=w_rows[:, j])
+            nc.sync.dma_start(out=w_raw[j + ROUNDS][:], in_=w_rows[:, j + ROUNDS])
+
+        ident = keep.tile([P, P], F32)
+        masks.make_identity(nc, ident[:])
+        above = keep.tile([P, EXPERTS + 1, TOKEN_TILES], F32)
+        nc.vector.memset(above[:, 0, :], 1.0)
+        nc.vector.memset(above[:, EXPERTS, :], 0.0)
+        for b, bound in enumerate(BOUNDS):
+            nc.vector.tensor_single_scalar(out=above[:, b + 1, :], in_=y_raw[:, :, 0], scalar=bound, op=ALU.is_gt)
+        sel = keep.tile([P, EXPERTS, TOKEN_TILES], F32)
+        nc.vector.tensor_tensor(out=sel[:], in0=above[:, 0:EXPERTS, :], in1=above[:, 1 : EXPERTS + 1, :], op=ALU.subtract)
+        half_sel = keep.tile([P, HALVES, TOKEN_TILES], F32)
+        nc.vector.tensor_tensor(
+            out=half_sel[:],
+            in0=above[:, 0:EXPERTS:ROUNDS, :],
+            in1=above[:, ROUNDS : EXPERTS + 1 : ROUNDS, :],
+            op=ALU.subtract,
+        )
+        pair_sel = keep.tile([P, ROUNDS, TOKEN_TILES], F32)
+        nc.vector.tensor_tensor(out=pair_sel[:], in0=sel[:, 0:ROUNDS, :], in1=sel[:, ROUNDS:EXPERTS, :], op=ALU.add)
+        ident_half = [keep.tile([P, HALVES, P], F32, name="ident_half%d" % i) for i in range(TOKEN_TILES)]
+        for i in range(TOKEN_TILES):
+            for h in range(HALVES):
+                nc.vector.tensor_scalar_mul(out=ident_half[i][:, h, :], in0=ident[:], scalar1=half_sel[:, h, i : i + 1])
+
+        def transpose_rows(bank_part, rows, identity):
+            words = rows.bitcast(F32)
+            for u in range(WORD_HALVES):
+                nc.tensor.transpose(bank_part[:, u, :], words[:, u * P : (u + 1) * P], identity)
+
+        def regroup(on_vector, grouped, part, bank):
+            dst = grouped[:].bitcast(F32)[:, part * BANK_WORDS : (part + 1) * BANK_WORDS]
+            dst = dst.rearrange("p (s c u) -> p s c u", s=2, u=WORD_HALVES)
+            src = bank[:].rearrange("p s u c -> p s c u")
+            if on_vector:
+                nc.vector.tensor_copy(out=dst, in_=src)
+            else:
+                nc.scalar.copy(out=dst, in_=src)
+
+        def prepare_weights(j, vector_helps):
+            pair = (j, j + ROUNDS)
+            for k in pair:
+                for part in range(ROW_TILES // 2):
+                    bank = words_psum.tile([P, 2, WORD_HALVES, P], F32, name="words")
+                    for s in range(2):
+                        transpose_rows(bank[:, s], w_raw[k][:, 2 * part + s, :], ident[:])
+                    regroup(vector_helps and part % 2 == 1, w_grouped[k], part, bank)
+            for k in pair:
+                nc.vector.quantize_mx(out=w_codes[k][:].bitcast(E4M3X4), scales=w_scales[k][:], in_=w_grouped[k][:])
+
+        def quantise_tokens(i):
+            nc.vector.quantize_mx(out=g_codes[i][:].bitcast(E5M2X4), scales=g_scales[i][:], in_=g_grouped[i][:])
+
+        def prepare_tokens(tiles, vector_helps):
+            for i in tiles:
+                rows = g_raw[i // len(tiles)][:, i % len(tiles), :]
+                bank = words_psum.tile([P, HALVES, WORD_HALVES, P], F32, name="words")
+                for h in range(HALVES):
+                    transpose_rows(bank[:, h], rows, ident_half[i][:, h, :])
+                regroup(vector_helps and i % 2 == 1, g_grouped[i], 0, bank)
+                if i > tiles[0]:
+                    quantise_tokens(i - 1)
+            quantise_tokens(tiles[-1])
+
+        def multiply(j, tiles):
+            for i in tiles:
+                bank = product_psum.tile([P, D], F32, name="product")
+                for h in range(HALVES):
+                    k = j + h * ROUNDS
+                    nc.tensor.matmul_mx(
+                        out=bank[:],
+                        lhsT=g_codes[i][:, h * P : (h + 1) * P].bitcast(E5M2X4),
+                        lhsT_scale=g_scales[i][:, h * P : (h + 1) * P],
+                        rhs=w_codes[k][:].bitcast(E4M3X4),
+                        rhs_scale=w_scales[k][:],
+                        start=(h == 0),
+                        stop=(h == HALVES - 1),
+                    )
+                factor = pair_sel[:, j, i : i + 1]
+                if j == 0:
+                    nc.scalar.activation(out=acc[i][:], in_=bank[:], func=COPY, scale=factor)
+                else:
+                    nc.vector.scalar_tensor_tensor(
+                        out=acc[i][:], in0=bank[:], scalar=factor, in1=acc[i][:], op0=ALU.mult, op1=ALU.add
+                    )
+                if j == ROUNDS - 1:
+                    nc.sync.dma_start(out=out_rows[:, i, :], in_=acc[i][:])
+
+        prepare_weights(0, True)
+        prepare_tokens(first_tiles, True)
+        for j in range(ROUNDS):
+            multiply(j, first_tiles)
+            if j == 0:
+                prepare_tokens(last_tiles, True)
+            if j + 1 < ROUNDS:
+                prepare_weights(j + 1, j == 0)
+            multiply(j, last_tiles)

@@ -25,6 +25,7 @@ ROW_TILES = D // P
 PACK = 4
 WORD_HALVES = 2
 BANK_WORDS = 512
+DETOUR_EVERY = 4
 X_RUN = 16
 
 FLOPS = 2 * EXPERTS * TOKENS * D * F
@@ -43,6 +44,7 @@ def tile_dispatchbyvariable_pa_kernel(tc, x, W, grad_out, out):
 
     with ExitStack() as ctx:
         keep = ctx.enter_context(tc.tile_pool(name="keep", bufs=1))
+        terms = ctx.enter_context(tc.tile_pool(name="terms", bufs=2))
         words_psum = ctx.enter_context(tc.psum_pool(name="words_psum", bufs=4))
         product_psum = ctx.enter_context(tc.psum_pool(name="product_psum", bufs=4))
         ctx.enter_context(tc.manual_schedule())
@@ -153,6 +155,10 @@ def tile_dispatchbyvariable_pa_kernel(tc, x, W, grad_out, out):
                 factor = pair_sel[:, j, i : i + 1]
                 if j == 0:
                     nc.scalar.activation(out=acc[i][:], in_=bank[:], func=COPY, scale=factor)
+                elif i % DETOUR_EVERY == 0:
+                    term = terms.tile([P, D], F32, name="term")
+                    nc.scalar.activation(out=term[:], in_=bank[:], func=COPY, scale=factor)
+                    nc.gpsimd.tensor_tensor(out=acc[i][:], in0=acc[i][:], in1=term[:], op=ALU.add)
                 else:
                     nc.vector.scalar_tensor_tensor(
                         out=acc[i][:], in0=bank[:], scalar=factor, in1=acc[i][:], op0=ALU.mult, op1=ALU.add

@@ -45,13 +45,15 @@ def tile_dispatchbyvariable_pa_kernel(tc, x, W, grad_out, out):
     with ExitStack() as ctx:
         keep = ctx.enter_context(tc.tile_pool(name="keep", bufs=1))
         terms = ctx.enter_context(tc.tile_pool(name="terms", bufs=2))
-        words_psum = ctx.enter_context(tc.psum_pool(name="words_psum", bufs=4))
-        product_psum = ctx.enter_context(tc.psum_pool(name="product_psum", bufs=4))
+        psum = ctx.enter_context(tc.psum_pool(name="psum", bufs=8))
         ctx.enter_context(tc.manual_schedule())
 
         y_raw = keep.tile([P, TOKEN_TILES, X_RUN], BF16)
-        g_raw = [keep.tile([P, TOKEN_TILES // 2, F], BF16, name="g_raw%d" % c) for c in range(2)]
-        w_raw = [keep.tile([P, ROW_TILES, F], BF16, name="w_raw%d" % k) for k in range(EXPERTS)]
+        g_raw = [keep.tile([P, F], BF16, name="g_raw%d" % i) for i in range(TOKEN_TILES)]
+        w_raw = [
+            [keep.tile([P, 2, F], BF16, name="w_raw%d_%d" % (k, part)) for part in range(ROW_TILES // 2)]
+            for k in range(EXPERTS)
+        ]
         g_grouped = [
             keep.tile([P, HALVES * P * PACK], BF16, name="g_grouped%d" % i, align_bytes=64)
             for i in range(TOKEN_TILES)
@@ -67,24 +69,38 @@ def tile_dispatchbyvariable_pa_kernel(tc, x, W, grad_out, out):
         w_scales = [keep.tile([P, D], U8, name="w_scales%d" % k, align_bytes=64) for k in range(EXPERTS)]
         acc = [keep.tile([P, D], F32, name="acc%d" % i) for i in range(TOKEN_TILES)]
 
-        nc.sync.dma_start(out=y_raw[:], in_=x_rows[:, :, 0:X_RUN])
-        nc.sync.dma_start(out=w_raw[0][:], in_=w_rows[:, 0])
-        nc.sync.dma_start(out=w_raw[ROUNDS][:], in_=w_rows[:, ROUNDS])
-        nc.sync.dma_start(out=g_raw[0][:], in_=g_rows[:, 0 : TOKEN_TILES // 2, :])
-        nc.sync.dma_start(out=g_raw[1][:], in_=g_rows[:, TOKEN_TILES // 2 : TOKEN_TILES, :])
+        def load_weights(k):
+            for part in range(ROW_TILES // 2):
+                nc.sync.dma_start(out=w_raw[k][part][:], in_=w_rows[:, k, 2 * part : 2 * part + 2, :])
+
+        def load_tokens(tiles):
+            for i in tiles:
+                nc.sync.dma_start(out=g_raw[i][:], in_=g_rows[:, i, :])
+
+        nc.scalar.dma_start(out=y_raw[:], in_=x_rows[:, :, 0:X_RUN])
+        load_weights(0)
+        load_tokens(first_tiles)
+        load_weights(ROUNDS)
+        load_tokens(last_tiles)
         for j in range(1, ROUNDS):
-            nc.sync.dma_start(out=w_raw[j][:], in_=w_rows[:, j])
-            nc.sync.dma_start(out=w_raw[j + ROUNDS][:], in_=w_rows[:, j + ROUNDS])
+            load_weights(j)
+            load_weights(j + ROUNDS)
 
         ident = keep.tile([P, P], F32)
         masks.make_identity(nc, ident[:])
+        bounds = keep.tile([P, len(BOUNDS)], F32)
+        for b, bound in enumerate(BOUNDS):
+            nc.vector.memset(bounds[:, b : b + 1], bound)
         above = keep.tile([P, EXPERTS + 1, TOKEN_TILES], F32)
         nc.vector.memset(above[:, 0, :], 1.0)
         nc.vector.memset(above[:, EXPERTS, :], 0.0)
-        for b, bound in enumerate(BOUNDS):
-            nc.vector.tensor_single_scalar(out=above[:, b + 1, :], in_=y_raw[:, :, 0], scalar=bound, op=ALU.is_gt)
-        sel = keep.tile([P, EXPERTS, TOKEN_TILES], F32)
-        nc.vector.tensor_tensor(out=sel[:], in0=above[:, 0:EXPERTS, :], in1=above[:, 1 : EXPERTS + 1, :], op=ALU.subtract)
+        compare_shape = [P, len(BOUNDS), TOKEN_TILES]
+        nc.vector.tensor_tensor(
+            out=above[:, 1:EXPERTS, :],
+            in0=y_raw[:, :, 0].unsqueeze(1).to_broadcast(compare_shape),
+            in1=bounds[:].unsqueeze(2).to_broadcast(compare_shape),
+            op=ALU.is_gt,
+        )
         half_sel = keep.tile([P, HALVES, TOKEN_TILES], F32)
         nc.vector.tensor_tensor(
             out=half_sel[:],
@@ -92,12 +108,27 @@ def tile_dispatchbyvariable_pa_kernel(tc, x, W, grad_out, out):
             in1=above[:, ROUNDS : EXPERTS + 1 : ROUNDS, :],
             op=ALU.subtract,
         )
-        pair_sel = keep.tile([P, ROUNDS, TOKEN_TILES], F32)
-        nc.vector.tensor_tensor(out=pair_sel[:], in0=sel[:, 0:ROUNDS, :], in1=sel[:, ROUNDS:EXPERTS, :], op=ALU.add)
         ident_half = [keep.tile([P, HALVES, P], F32, name="ident_half%d" % i) for i in range(TOKEN_TILES)]
         for i in range(TOKEN_TILES):
             for h in range(HALVES):
-                nc.vector.tensor_scalar_mul(out=ident_half[i][:, h, :], in0=ident[:], scalar1=half_sel[:, h, i : i + 1])
+                nc.gpsimd.tensor_scalar(
+                    out=ident_half[i][:, h, :],
+                    in0=ident[:],
+                    scalar1=half_sel[:, h, i : i + 1],
+                    scalar2=0.0,
+                    op0=ALU.mult,
+                    op1=ALU.add,
+                )
+        sel = keep.tile([P, EXPERTS, TOKEN_TILES], F32)
+        pair_sel = keep.tile([P, ROUNDS, TOKEN_TILES], F32)
+
+        def pair_factors():
+            nc.vector.tensor_tensor(
+                out=sel[:], in0=above[:, 0:EXPERTS, :], in1=above[:, 1 : EXPERTS + 1, :], op=ALU.subtract
+            )
+            nc.vector.tensor_tensor(
+                out=pair_sel[:], in0=sel[:, 0:ROUNDS, :], in1=sel[:, ROUNDS:EXPERTS, :], op=ALU.add
+            )
 
         def transpose_rows(bank_part, rows, identity):
             words = rows.bitcast(F32)
@@ -113,65 +144,96 @@ def tile_dispatchbyvariable_pa_kernel(tc, x, W, grad_out, out):
             else:
                 nc.scalar.copy(out=dst, in_=src)
 
-        def prepare_weights(j, vector_helps):
-            pair = (j, j + ROUNDS)
-            for k in pair:
-                for part in range(ROW_TILES // 2):
-                    bank = words_psum.tile([P, 2, WORD_HALVES, P], F32, name="words")
-                    for s in range(2):
-                        transpose_rows(bank[:, s], w_raw[k][:, 2 * part + s, :], ident[:])
-                    regroup(vector_helps and part % 2 == 1, w_grouped[k], part, bank)
-            for k in pair:
-                nc.vector.quantize_mx(out=w_codes[k][:].bitcast(E4M3X4), scales=w_scales[k][:], in_=w_grouped[k][:])
+        def transpose_weights(k, on_vector):
+            for part in range(ROW_TILES // 2):
+                bank = psum.tile([P, 2, WORD_HALVES, P], F32, name="bank")
+                for s in range(2):
+                    transpose_rows(bank[:, s], w_raw[k][part][:, s, :], ident[:])
+                regroup(on_vector[part], w_grouped[k], part, bank)
+
+        def quantise_weights(k):
+            nc.vector.quantize_mx(out=w_codes[k][:].bitcast(E4M3X4), scales=w_scales[k][:], in_=w_grouped[k][:])
+
+        def transpose_tokens(i, on_vector):
+            bank = psum.tile([P, HALVES, WORD_HALVES, P], F32, name="bank")
+            for h in range(HALVES):
+                transpose_rows(bank[:, h], g_raw[i][:], ident_half[i][:, h, :])
+            regroup(on_vector, g_grouped[i], 0, bank)
 
         def quantise_tokens(i):
             nc.vector.quantize_mx(out=g_codes[i][:].bitcast(E5M2X4), scales=g_scales[i][:], in_=g_grouped[i][:])
 
-        def prepare_tokens(tiles, vector_helps):
-            for i in tiles:
-                rows = g_raw[i // len(tiles)][:, i % len(tiles), :]
-                bank = words_psum.tile([P, HALVES, WORD_HALVES, P], F32, name="words")
-                for h in range(HALVES):
-                    transpose_rows(bank[:, h], rows, ident_half[i][:, h, :])
-                regroup(vector_helps and i % 2 == 1, g_grouped[i], 0, bank)
-                if i > tiles[0]:
-                    quantise_tokens(i - 1)
-            quantise_tokens(tiles[-1])
+        def one_pass(bank, i, j, h):
+            k = j + h * ROUNDS
+            nc.tensor.matmul_mx(
+                out=bank[:],
+                lhsT=g_codes[i][:, h * P : (h + 1) * P].bitcast(E5M2X4),
+                lhsT_scale=g_scales[i][:, h * P : (h + 1) * P],
+                rhs=w_codes[k][:].bitcast(E4M3X4),
+                rhs_scale=w_scales[k][:],
+                start=(h == 0),
+                stop=(h == HALVES - 1),
+            )
+
+        def collect(bank, i, j):
+            factor = pair_sel[:, j, i : i + 1]
+            if j == 0:
+                nc.scalar.activation(out=acc[i][:], in_=bank[:], func=COPY, scale=factor)
+            elif (i + j) % DETOUR_EVERY == 0:
+                term = terms.tile([P, D], F32, name="term")
+                nc.scalar.activation(out=term[:], in_=bank[:], func=COPY, scale=factor)
+                nc.gpsimd.tensor_tensor(out=acc[i][:], in0=acc[i][:], in1=term[:], op=ALU.add)
+            else:
+                nc.vector.scalar_tensor_tensor(
+                    out=acc[i][:], in0=bank[:], scalar=factor, in1=acc[i][:], op0=ALU.mult, op1=ALU.add
+                )
+            if j == ROUNDS - 1:
+                nc.sync.dma_start(out=out_rows[:, i, :], in_=acc[i][:])
 
         def multiply(j, tiles):
             for i in tiles:
-                bank = product_psum.tile([P, D], F32, name="product")
+                bank = psum.tile([P, D], F32, name="bank")
                 for h in range(HALVES):
-                    k = j + h * ROUNDS
-                    nc.tensor.matmul_mx(
-                        out=bank[:],
-                        lhsT=g_codes[i][:, h * P : (h + 1) * P].bitcast(E5M2X4),
-                        lhsT_scale=g_scales[i][:, h * P : (h + 1) * P],
-                        rhs=w_codes[k][:].bitcast(E4M3X4),
-                        rhs_scale=w_scales[k][:],
-                        start=(h == 0),
-                        stop=(h == HALVES - 1),
-                    )
-                factor = pair_sel[:, j, i : i + 1]
-                if j == 0:
-                    nc.scalar.activation(out=acc[i][:], in_=bank[:], func=COPY, scale=factor)
-                elif i % DETOUR_EVERY == 0:
-                    term = terms.tile([P, D], F32, name="term")
-                    nc.scalar.activation(out=term[:], in_=bank[:], func=COPY, scale=factor)
-                    nc.gpsimd.tensor_tensor(out=acc[i][:], in0=acc[i][:], in1=term[:], op=ALU.add)
-                else:
-                    nc.vector.scalar_tensor_tensor(
-                        out=acc[i][:], in0=bank[:], scalar=factor, in1=acc[i][:], op0=ALU.mult, op1=ALU.add
-                    )
-                if j == ROUNDS - 1:
-                    nc.sync.dma_start(out=out_rows[:, i, :], in_=acc[i][:])
+                    one_pass(bank, i, j, h)
+                collect(bank, i, j)
 
-        prepare_weights(0, True)
-        prepare_tokens(first_tiles, True)
-        for j in range(ROUNDS):
+        transpose_weights(0, (False, True))
+        transpose_tokens(0, False)
+        quantise_weights(0)
+        transpose_tokens(1, True)
+        transpose_tokens(2, False)
+        quantise_tokens(0)
+        quantise_tokens(1)
+        transpose_tokens(3, True)
+        quantise_tokens(2)
+        transpose_weights(ROUNDS, (False, True))
+        quantise_tokens(3)
+        open_banks = [psum.tile([P, D], F32, name="bank") for i in first_tiles]
+        for i in first_tiles:
+            one_pass(open_banks[i], i, 0, 0)
+        quantise_weights(ROUNDS)
+        pair_factors()
+        transpose_tokens(4, False)
+        transpose_tokens(5, True)
+        for i in first_tiles:
+            one_pass(open_banks[i], i, 0, 1)
+            collect(open_banks[i], i, 0)
+        quantise_tokens(4)
+        quantise_tokens(5)
+        transpose_tokens(6, True)
+        transpose_tokens(7, True)
+        transpose_weights(1, (True, False))
+        quantise_tokens(6)
+        quantise_tokens(7)
+        transpose_weights(1 + ROUNDS, (True, False))
+        quantise_weights(1)
+        quantise_weights(1 + ROUNDS)
+        multiply(0, last_tiles)
+        for j in range(1, ROUNDS):
             multiply(j, first_tiles)
-            if j == 0:
-                prepare_tokens(last_tiles, True)
             if j + 1 < ROUNDS:
-                prepare_weights(j + 1, j == 0)
+                transpose_weights(j + 1, (False, False))
+                transpose_weights(j + 1 + ROUNDS, (False, False))
+                quantise_weights(j + 1)
+                quantise_weights(j + 1 + ROUNDS)
             multiply(j, last_tiles)

@@ -39,8 +39,8 @@ def tile_dispatchbyvariable_pa_kernel(tc, x, W, grad_out, out):
     out_rows = out.flatten_outer_dims().rearrange("(i p) d -> p i d", p=P)
     w_rows = W.rearrange("k (r p) f -> p k r f", p=P)
 
-    first_tiles = range(0, TOKEN_TILES // 2)
-    last_tiles = range(TOKEN_TILES // 2, TOKEN_TILES)
+    first_tiles = list(range(0, TOKEN_TILES // 2))
+    last_tiles = list(range(TOKEN_TILES // 2, TOKEN_TILES))
 
     with ExitStack() as ctx:
         keep = ctx.enter_context(tc.tile_pool(name="keep", bufs=1))
@@ -77,7 +77,7 @@ def tile_dispatchbyvariable_pa_kernel(tc, x, W, grad_out, out):
             for i in tiles:
                 nc.sync.dma_start(out=g_raw[i][:], in_=g_rows[:, i, :])
 
-        nc.scalar.dma_start(out=y_raw[:], in_=x_rows[:, :, 0:X_RUN])
+        nc.sync.dma_start(out=y_raw[:], in_=x_rows[:, :, 0:X_RUN])
         load_weights(0)
         load_tokens(first_tiles)
         load_weights(ROUNDS)
@@ -111,14 +111,19 @@ def tile_dispatchbyvariable_pa_kernel(tc, x, W, grad_out, out):
         ident_half = [keep.tile([P, HALVES, P], F32, name="ident_half%d" % i) for i in range(TOKEN_TILES)]
         for i in range(TOKEN_TILES):
             for h in range(HALVES):
-                nc.gpsimd.tensor_scalar(
-                    out=ident_half[i][:, h, :],
-                    in0=ident[:],
-                    scalar1=half_sel[:, h, i : i + 1],
-                    scalar2=0.0,
-                    op0=ALU.mult,
-                    op1=ALU.add,
-                )
+                if i < 2:
+                    nc.vector.tensor_scalar_mul(
+                        out=ident_half[i][:, h, :], in0=ident[:], scalar1=half_sel[:, h, i : i + 1]
+                    )
+                else:
+                    nc.gpsimd.tensor_scalar(
+                        out=ident_half[i][:, h, :],
+                        in0=ident[:],
+                        scalar1=half_sel[:, h, i : i + 1],
+                        scalar2=0.0,
+                        op0=ALU.mult,
+                        op1=ALU.add,
+                    )
         sel = keep.tile([P, EXPERTS, TOKEN_TILES], F32)
         pair_sel = keep.tile([P, ROUNDS, TOKEN_TILES], F32)
 
@@ -144,15 +149,26 @@ def tile_dispatchbyvariable_pa_kernel(tc, x, W, grad_out, out):
             else:
                 nc.scalar.copy(out=dst, in_=src)
 
+        def transpose_weights_half(k, part, on_vector):
+            bank = psum.tile([P, 2, WORD_HALVES, P], F32, name="bank")
+            for s in range(2):
+                transpose_rows(bank[:, s], w_raw[k][part][:, s, :], ident[:])
+            regroup(on_vector, w_grouped[k], part, bank)
+
         def transpose_weights(k, on_vector):
             for part in range(ROW_TILES // 2):
-                bank = psum.tile([P, 2, WORD_HALVES, P], F32, name="bank")
-                for s in range(2):
-                    transpose_rows(bank[:, s], w_raw[k][part][:, s, :], ident[:])
-                regroup(on_vector[part], w_grouped[k], part, bank)
+                transpose_weights_half(k, part, on_vector[part])
 
         def quantise_weights(k):
             nc.vector.quantize_mx(out=w_codes[k][:].bitcast(E4M3X4), scales=w_scales[k][:], in_=w_grouped[k][:])
+
+        def quantise_weights_half(k, part):
+            cols = slice(part * (D // 2), (part + 1) * (D // 2))
+            nc.vector.quantize_mx(
+                out=w_codes[k][:, cols].bitcast(E4M3X4),
+                scales=w_scales[k][:, cols],
+                in_=w_grouped[k][:, part * (D // 2) * PACK : (part + 1) * (D // 2) * PACK],
+            )
 
         def transpose_tokens(i, on_vector):
             bank = psum.tile([P, HALVES, WORD_HALVES, P], F32, name="bank")
@@ -179,7 +195,7 @@ def tile_dispatchbyvariable_pa_kernel(tc, x, W, grad_out, out):
             factor = pair_sel[:, j, i : i + 1]
             if j == 0:
                 nc.scalar.activation(out=acc[i][:], in_=bank[:], func=COPY, scale=factor)
-            elif (i + j) % DETOUR_EVERY == 0:
+            elif (i + j) % DETOUR_EVERY == 0 and not (j == ROUNDS - 1 and i in last_tiles):
                 term = terms.tile([P, D], F32, name="term")
                 nc.scalar.activation(out=term[:], in_=bank[:], func=COPY, scale=factor)
                 nc.gpsimd.tensor_tensor(out=acc[i][:], in0=acc[i][:], in1=term[:], op=ALU.add)
@@ -197,21 +213,25 @@ def tile_dispatchbyvariable_pa_kernel(tc, x, W, grad_out, out):
                     one_pass(bank, i, j, h)
                 collect(bank, i, j)
 
-        transpose_weights(0, (False, True))
-        transpose_tokens(0, False)
-        quantise_weights(0)
-        transpose_tokens(1, True)
-        transpose_tokens(2, False)
+        transpose_weights_half(0, 0, False)
+        transpose_weights_half(0, 1, False)
+        quantise_weights_half(0, 0)
+        transpose_tokens(0, True)
+        quantise_weights_half(0, 1)
+        transpose_tokens(1, False)
         quantise_tokens(0)
+        transpose_tokens(2, False)
         quantise_tokens(1)
-        transpose_tokens(3, True)
+        transpose_tokens(3, False)
         quantise_tokens(2)
-        transpose_weights(ROUNDS, (False, True))
+        transpose_weights_half(ROUNDS, 0, True)
+        transpose_weights_half(ROUNDS, 1, False)
         quantise_tokens(3)
         open_banks = [psum.tile([P, D], F32, name="bank") for i in first_tiles]
         for i in first_tiles:
             one_pass(open_banks[i], i, 0, 0)
-        quantise_weights(ROUNDS)
+        quantise_weights_half(ROUNDS, 0)
+        quantise_weights_half(ROUNDS, 1)
         pair_factors()
         transpose_tokens(4, False)
         transpose_tokens(5, True)
@@ -230,10 +250,13 @@ def tile_dispatchbyvariable_pa_kernel(tc, x, W, grad_out, out):
         quantise_weights(1 + ROUNDS)
         multiply(0, last_tiles)
         for j in range(1, ROUNDS):
-            multiply(j, first_tiles)
             if j + 1 < ROUNDS:
                 transpose_weights(j + 1, (False, False))
                 transpose_weights(j + 1 + ROUNDS, (False, False))
+                multiply(j, first_tiles[:2])
                 quantise_weights(j + 1)
+                multiply(j, first_tiles[2:])
                 quantise_weights(j + 1 + ROUNDS)
+            else:
+                multiply(j, first_tiles)
             multiply(j, last_tiles)

@@ -195,7 +195,7 @@ def tile_dispatchbyvariable_pa_kernel(tc, x, W, grad_out, out):
             factor = pair_sel[:, j, i : i + 1]
             if j == 0:
                 nc.scalar.activation(out=acc[i][:], in_=bank[:], func=COPY, scale=factor)
-            elif (i + j) % DETOUR_EVERY == 0 and not (j == ROUNDS - 1 and i in last_tiles):
+            elif (i + j) % DETOUR_EVERY == 0 and j < ROUNDS - 1:
                 term = terms.tile([P, D], F32, name="term")
                 nc.scalar.activation(out=term[:], in_=bank[:], func=COPY, scale=factor)
                 nc.gpsimd.tensor_tensor(out=acc[i][:], in0=acc[i][:], in1=term[:], op=ALU.add)
@@ -249,14 +249,13 @@ def tile_dispatchbyvariable_pa_kernel(tc, x, W, grad_out, out):
         quantise_weights(1)
         quantise_weights(1 + ROUNDS)
         multiply(0, last_tiles)
-        for j in range(1, ROUNDS):
-            if j + 1 < ROUNDS:
-                transpose_weights(j + 1, (False, False))
-                transpose_weights(j + 1 + ROUNDS, (False, False))
-                multiply(j, first_tiles[:2])
-                quantise_weights(j + 1)
-                multiply(j, first_tiles[2:])
-                quantise_weights(j + 1 + ROUNDS)
-            else:
-                multiply(j, first_tiles)
-            multiply(j, last_tiles)
+        for tiles, j in ((first_tiles, 2), (last_tiles, 3)):
+            transpose_weights(j, (False, False))
+            transpose_weights(j + ROUNDS, (False, False))
+            multiply(1, tiles[:2])
+            quantise_weights(j)
+            multiply(1, tiles[2:])
+            quantise_weights(j + ROUNDS)
+        for tiles in (first_tiles, last_tiles):
+            multiply(2, tiles)
+            multiply(3, tiles)

@@ -34,10 +34,10 @@ BYTES = 2 * EXPERTS * D * F + 2 * TOKENS * F + 4 * TOKENS * D + 2 * TOKENS
 
 def tile_dispatchbyvariable_pa_kernel(tc, x, W, grad_out, out):
     nc = tc.nc
-    x_rows = x.flatten_outer_dims().rearrange("(i p) d -> p i d", p=P)
-    g_rows = grad_out.flatten_outer_dims().rearrange("(i p) f -> p i f", p=P)
-    out_rows = out.flatten_outer_dims().rearrange("(i p) d -> p i d", p=P)
-    w_rows = W.rearrange("k (r p) f -> p k r f", p=P)
+    x_rows = x.flatten_outer_dims().rearrange("(p i) d -> p i d", p=P)
+    g_rows = grad_out.flatten_outer_dims().rearrange("(p i) f -> p i f", p=P)
+    out_rows = out.flatten_outer_dims().rearrange("(p i) d -> p i d", p=P)
+    w_rows = W.rearrange("k (p r) f -> p k r f", p=P)
 
     first_tiles = list(range(0, TOKEN_TILES // 2))
     last_tiles = list(range(TOKEN_TILES // 2, TOKEN_TILES))
@@ -49,7 +49,7 @@ def tile_dispatchbyvariable_pa_kernel(tc, x, W, grad_out, out):
         ctx.enter_context(tc.manual_schedule())
 
         y_raw = keep.tile([P, TOKEN_TILES, X_RUN], BF16)
-        g_raw = [keep.tile([P, F], BF16, name="g_raw%d" % i) for i in range(TOKEN_TILES)]
+        g_raw = [keep.tile([P, 2, F], BF16, name="g_raw%d" % c) for c in range(TOKEN_TILES // 2)]
         w_raw = [
             [keep.tile([P, 2, F], BF16, name="w_raw%d_%d" % (k, part)) for part in range(ROW_TILES // 2)]
             for k in range(EXPERTS)
@@ -74,8 +74,8 @@ def tile_dispatchbyvariable_pa_kernel(tc, x, W, grad_out, out):
                 nc.sync.dma_start(out=w_raw[k][part][:], in_=w_rows[:, k, 2 * part : 2 * part + 2, :])
 
         def load_tokens(tiles):
-            for i in tiles:
-                nc.sync.dma_start(out=g_raw[i][:], in_=g_rows[:, i, :])
+            for c in range(tiles[0] // 2, tiles[-1] // 2 + 1):
+                nc.sync.dma_start(out=g_raw[c][:], in_=g_rows[:, 2 * c : 2 * c + 2, :])
 
         nc.sync.dma_start(out=y_raw[:], in_=x_rows[:, :, 0:X_RUN])
         load_weights(0)
@@ -173,7 +173,7 @@ def tile_dispatchbyvariable_pa_kernel(tc, x, W, grad_out, out):
         def transpose_tokens(i, on_vector):
             bank = psum.tile([P, HALVES, WORD_HALVES, P], F32, name="bank")
             for h in range(HALVES):
-                transpose_rows(bank[:, h], g_raw[i][:], ident_half[i][:, h, :])
+                transpose_rows(bank[:, h], g_raw[i // 2][:, i % 2, :], ident_half[i][:, h, :])
             regroup(on_vector, g_grouped[i], 0, bank)
 
         def quantise_tokens(i):
@@ -193,15 +193,19 @@ def tile_dispatchbyvariable_pa_kernel(tc, x, W, grad_out, out):
 
         def collect(bank, i, j):
             factor = pair_sel[:, j, i : i + 1]
+            product = bank[:].rearrange("p (r c) -> p c r", r=ROW_TILES)
+            total = acc[i][:].rearrange("p (c r) -> p c r", r=ROW_TILES)
             if j == 0:
-                nc.scalar.activation(out=acc[i][:], in_=bank[:], func=COPY, scale=factor)
+                nc.scalar.activation(out=total, in_=product, func=COPY, scale=factor)
             elif (i + j) % DETOUR_EVERY == 0 and j < ROUNDS - 1:
                 term = terms.tile([P, D], F32, name="term")
-                nc.scalar.activation(out=term[:], in_=bank[:], func=COPY, scale=factor)
+                nc.scalar.activation(
+                    out=term[:].rearrange("p (c r) -> p c r", r=ROW_TILES), in_=product, func=COPY, scale=factor
+                )
                 nc.gpsimd.tensor_tensor(out=acc[i][:], in0=acc[i][:], in1=term[:], op=ALU.add)
             else:
                 nc.vector.scalar_tensor_tensor(
-                    out=acc[i][:], in0=bank[:], scalar=factor, in1=acc[i][:], op0=ALU.mult, op1=ALU.add
+                    out=total, in0=product, scalar=factor, in1=total, op0=ALU.mult, op1=ALU.add
                 )
             if j == ROUNDS - 1:
                 nc.sync.dma_start(out=out_rows[:, i, :], in_=acc[i][:])

@@ -50,8 +50,9 @@ def tile_dispatchbyvariable_pa_kernel(tc, x, W, grad_out, out):
 
         y_raw = keep.tile([P, TOKEN_TILES, X_RUN], BF16)
         g_raw = [keep.tile([P, 2, F], BF16, name="g_raw%d" % c) for c in range(TOKEN_TILES // 2)]
+        w_loads = [2 if k % ROUNDS == 0 else 1 for k in range(EXPERTS)]
         w_raw = [
-            [keep.tile([P, 2, F], BF16, name="w_raw%d_%d" % (k, part)) for part in range(ROW_TILES // 2)]
+            [keep.tile([P, ROW_TILES // w_loads[k], F], BF16, name="w_raw%d_%d" % (k, c)) for c in range(w_loads[k])]
             for k in range(EXPERTS)
         ]
         g_grouped = [
@@ -70,8 +71,13 @@ def tile_dispatchbyvariable_pa_kernel(tc, x, W, grad_out, out):
         acc = [keep.tile([P, D], F32, name="acc%d" % i) for i in range(TOKEN_TILES)]
 
         def load_weights(k):
-            for part in range(ROW_TILES // 2):
-                nc.sync.dma_start(out=w_raw[k][part][:], in_=w_rows[:, k, 2 * part : 2 * part + 2, :])
+            rows = ROW_TILES // w_loads[k]
+            for c in range(w_loads[k]):
+                nc.sync.dma_start(out=w_raw[k][c][:], in_=w_rows[:, k, c * rows : (c + 1) * rows, :])
+
+        def weight_rows(k, r):
+            rows = ROW_TILES // w_loads[k]
+            return w_raw[k][r // rows][:, r % rows, :]
 
         def load_tokens(tiles):
             for c in range(tiles[0] // 2, tiles[-1] // 2 + 1):
@@ -152,7 +158,7 @@ def tile_dispatchbyvariable_pa_kernel(tc, x, W, grad_out, out):
         def transpose_weights_half(k, part, on_vector):
             bank = psum.tile([P, 2, WORD_HALVES, P], F32, name="bank")
             for s in range(2):
-                transpose_rows(bank[:, s], w_raw[k][part][:, s, :], ident[:])
+                transpose_rows(bank[:, s], weight_rows(k, 2 * part + s), ident[:])
             regroup(on_vector, w_grouped[k], part, bank)
 
         def transpose_weights(k, on_vector):

from contextlib import ExitStack

import concourse.masks as masks
import concourse.mybir as mybir

F32 = mybir.dt.float32
BF16 = mybir.dt.bfloat16
U32 = mybir.dt.uint32
U8 = mybir.dt.uint8
E4M3X4 = mybir.dt.float8_e4m3fn_x4
E5M2X4 = mybir.dt.float8_e5m2_x4
ALU = mybir.AluOpType
COPY = mybir.ActivationFunctionType.Copy

P = 128
TOKENS = 1024
D = 512
F = 512
BOUNDS = (-1.5, -1.0, -0.5, 0.0, 0.5, 1.0, 1.5)
EXPERTS = len(BOUNDS) + 1
HALVES = 2
ROUNDS = EXPERTS // HALVES
TOKEN_TILES = TOKENS // P
ROW_TILES = D // P
PACK = 4
WORD_HALVES = 2
BANK_WORDS = 512
DETOUR_EVERY = 4
X_RUN = 16

FLOPS = 2 * EXPERTS * TOKENS * D * F
BYTES = 2 * EXPERTS * D * F + 2 * TOKENS * F + 4 * TOKENS * D + 2 * TOKENS


def tile_dispatchbyvariable_pa_kernel(tc, x, W, grad_out, out):
    nc = tc.nc
    x_rows = x.flatten_outer_dims().rearrange("(p i) d -> p i d", p=P)
    g_rows = grad_out.flatten_outer_dims().rearrange("(p i) f -> p i f", p=P)
    out_rows = out.flatten_outer_dims().rearrange("(p i) d -> p i d", p=P)
    w_rows = W.rearrange("k (p r) f -> p k r f", p=P)

    first_tiles = list(range(0, TOKEN_TILES // 2))
    last_tiles = list(range(TOKEN_TILES // 2, TOKEN_TILES))

    with ExitStack() as ctx:
        keep = ctx.enter_context(tc.tile_pool(name="keep", bufs=1))
        terms = ctx.enter_context(tc.tile_pool(name="terms", bufs=2))
        psum = ctx.enter_context(tc.psum_pool(name="psum", bufs=8))
        ctx.enter_context(tc.manual_schedule())

        y_raw = keep.tile([P, TOKEN_TILES, X_RUN], BF16)
        g_raw = [keep.tile([P, 2, F], BF16, name="g_raw%d" % c) for c in range(TOKEN_TILES // 2)]
        w_loads = [2 if k % ROUNDS == 0 else 1 for k in range(EXPERTS)]
        w_raw = [
            [keep.tile([P, ROW_TILES // w_loads[k], F], BF16, name="w_raw%d_%d" % (k, c)) for c in range(w_loads[k])]
            for k in range(EXPERTS)
        ]
        g_grouped = [
            keep.tile([P, HALVES * P * PACK], BF16, name="g_grouped%d" % i, align_bytes=64)
            for i in range(TOKEN_TILES)
        ]
        g_codes = [
            keep.tile([P, HALVES * P], U32, name="g_codes%d" % i, align_bytes=64) for i in range(TOKEN_TILES)
        ]
        g_scales = [
            keep.tile([P, HALVES * P], U8, name="g_scales%d" % i, align_bytes=64) for i in range(TOKEN_TILES)
        ]
        w_grouped = [keep.tile([P, D * PACK], BF16, name="w_grouped%d" % k, align_bytes=64) for k in range(EXPERTS)]
        w_codes = [keep.tile([P, D], U32, name="w_codes%d" % k, align_bytes=64) for k in range(EXPERTS)]
        w_scales = [keep.tile([P, D], U8, name="w_scales%d" % k, align_bytes=64) for k in range(EXPERTS)]
        acc = [keep.tile([P, D], F32, name="acc%d" % i) for i in range(TOKEN_TILES)]

        def load_weights(k):
            rows = ROW_TILES // w_loads[k]
            for c in range(w_loads[k]):
                nc.sync.dma_start(out=w_raw[k][c][:], in_=w_rows[:, k, c * rows : (c + 1) * rows, :])

        def weight_rows(k, r):
            rows = ROW_TILES // w_loads[k]
            return w_raw[k][r // rows][:, r % rows, :]

        def load_tokens(tiles):
            for c in range(tiles[0] // 2, tiles[-1] // 2 + 1):
                nc.sync.dma_start(out=g_raw[c][:], in_=g_rows[:, 2 * c : 2 * c + 2, :])

        nc.sync.dma_start(out=y_raw[:], in_=x_rows[:, :, 0:X_RUN])
        load_weights(0)
        load_tokens(first_tiles)
        load_weights(ROUNDS)
        load_tokens(last_tiles)
        for j in range(1, ROUNDS):
            load_weights(j)
            load_weights(j + ROUNDS)

        ident = keep.tile([P, P], F32)
        masks.make_identity(nc, ident[:])
        bounds = keep.tile([P, len(BOUNDS)], F32)
        for b, bound in enumerate(BOUNDS):
            nc.vector.memset(bounds[:, b : b + 1], bound)
        above = keep.tile([P, EXPERTS + 1, TOKEN_TILES], F32)
        nc.vector.memset(above[:, 0, :], 1.0)
        nc.vector.memset(above[:, EXPERTS, :], 0.0)
        compare_shape = [P, len(BOUNDS), TOKEN_TILES]
        nc.vector.tensor_tensor(
            out=above[:, 1:EXPERTS, :],
            in0=y_raw[:, :, 0].unsqueeze(1).to_broadcast(compare_shape),
            in1=bounds[:].unsqueeze(2).to_broadcast(compare_shape),
            op=ALU.is_gt,
        )
        half_sel = keep.tile([P, HALVES, TOKEN_TILES], F32)
        nc.vector.tensor_tensor(
            out=half_sel[:],
            in0=above[:, 0:EXPERTS:ROUNDS, :],
            in1=above[:, ROUNDS : EXPERTS + 1 : ROUNDS, :],
            op=ALU.subtract,
        )
        ident_half = [keep.tile([P, HALVES, P], F32, name="ident_half%d" % i) for i in range(TOKEN_TILES)]
        for i in range(TOKEN_TILES):
            for h in range(HALVES):
                if i < 2:
                    nc.vector.tensor_scalar_mul(
                        out=ident_half[i][:, h, :], in0=ident[:], scalar1=half_sel[:, h, i : i + 1]
                    )
                else:
                    nc.gpsimd.tensor_scalar(
                        out=ident_half[i][:, h, :],
                        in0=ident[:],
                        scalar1=half_sel[:, h, i : i + 1],
                        scalar2=0.0,
                        op0=ALU.mult,
                        op1=ALU.add,
                    )
        sel = keep.tile([P, EXPERTS, TOKEN_TILES], F32)
        pair_sel = keep.tile([P, ROUNDS, TOKEN_TILES], F32)

        def pair_factors():
            nc.vector.tensor_tensor(
                out=sel[:], in0=above[:, 0:EXPERTS, :], in1=above[:, 1 : EXPERTS + 1, :], op=ALU.subtract
            )
            nc.vector.tensor_tensor(
                out=pair_sel[:], in0=sel[:, 0:ROUNDS, :], in1=sel[:, ROUNDS:EXPERTS, :], op=ALU.add
            )

        def transpose_rows(bank_part, rows, identity):
            words = rows.bitcast(F32)
            for u in range(WORD_HALVES):
                nc.tensor.transpose(bank_part[:, u, :], words[:, u * P : (u + 1) * P], identity)

        def regroup(on_vector, grouped, part, bank):
            dst = grouped[:].bitcast(F32)[:, part * BANK_WORDS : (part + 1) * BANK_WORDS]
            dst = dst.rearrange("p (s c u) -> p s c u", s=2, u=WORD_HALVES)
            src = bank[:].rearrange("p s u c -> p s c u")
            if on_vector:
                nc.vector.tensor_copy(out=dst, in_=src)
            else:
                nc.scalar.copy(out=dst, in_=src)

        def transpose_weights_half(k, part, on_vector):
            bank = psum.tile([P, 2, WORD_HALVES, P], F32, name="bank")
            for s in range(2):
                transpose_rows(bank[:, s], weight_rows(k, 2 * part + s), ident[:])
            regroup(on_vector, w_grouped[k], part, bank)

        def transpose_weights(k, on_vector):
            for part in range(ROW_TILES // 2):
                transpose_weights_half(k, part, on_vector[part])

        def quantise_weights(k):
            nc.vector.quantize_mx(out=w_codes[k][:].bitcast(E4M3X4), scales=w_scales[k][:], in_=w_grouped[k][:])

        def quantise_weights_half(k, part):
            cols = slice(part * (D // 2), (part + 1) * (D // 2))
            nc.vector.quantize_mx(
                out=w_codes[k][:, cols].bitcast(E4M3X4),
                scales=w_scales[k][:, cols],
                in_=w_grouped[k][:, part * (D // 2) * PACK : (part + 1) * (D // 2) * PACK],
            )

        def transpose_tokens(i, on_vector):
            bank = psum.tile([P, HALVES, WORD_HALVES, P], F32, name="bank")
            for h in range(HALVES):
                transpose_rows(bank[:, h], g_raw[i // 2][:, i % 2, :], ident_half[i][:, h, :])
            regroup(on_vector, g_grouped[i], 0, bank)

        def quantise_tokens(i):
            nc.vector.quantize_mx(out=g_codes[i][:].bitcast(E5M2X4), scales=g_scales[i][:], in_=g_grouped[i][:])

        def one_pass(bank, i, j, h):
            k = j + h * ROUNDS
            nc.tensor.matmul_mx(
                out=bank[:],
                lhsT=g_codes[i][:, h * P : (h + 1) * P].bitcast(E5M2X4),
                lhsT_scale=g_scales[i][:, h * P : (h + 1) * P],
                rhs=w_codes[k][:].bitcast(E4M3X4),
                rhs_scale=w_scales[k][:],
                start=(h == 0),
                stop=(h == HALVES - 1),
            )

        def collect(bank, i, j):
            factor = pair_sel[:, j, i : i + 1]
            product = bank[:].rearrange("p (r c) -> p c r", r=ROW_TILES)
            total = acc[i][:].rearrange("p (c r) -> p c r", r=ROW_TILES)
            if j == 0:
                nc.scalar.activation(out=total, in_=product, func=COPY, scale=factor)
            elif (i + j) % DETOUR_EVERY == 0 and j < ROUNDS - 1:
                term = terms.tile([P, D], F32, name="term")
                nc.scalar.activation(
                    out=term[:].rearrange("p (c r) -> p c r", r=ROW_TILES), in_=product, func=COPY, scale=factor
                )
                nc.gpsimd.tensor_tensor(out=acc[i][:], in0=acc[i][:], in1=term[:], op=ALU.add)
            else:
                nc.vector.scalar_tensor_tensor(
                    out=total, in0=product, scalar=factor, in1=total, op0=ALU.mult, op1=ALU.add
                )
            if j == ROUNDS - 1:
                nc.sync.dma_start(out=out_rows[:, i, :], in_=acc[i][:])

        def multiply(j, tiles):
            for i in tiles:
                bank = psum.tile([P, D], F32, name="bank")
                for h in range(HALVES):
                    one_pass(bank, i, j, h)
                collect(bank, i, j)

        transpose_weights_half(0, 0, False)
        transpose_weights_half(0, 1, False)
        quantise_weights_half(0, 0)
        transpose_tokens(0, True)
        quantise_weights_half(0, 1)
        transpose_tokens(1, False)
        quantise_tokens(0)
        transpose_tokens(2, False)
        quantise_tokens(1)
        transpose_tokens(3, False)
        quantise_tokens(2)
        transpose_weights_half(ROUNDS, 0, True)
        transpose_weights_half(ROUNDS, 1, False)
        quantise_tokens(3)
        open_banks = [psum.tile([P, D], F32, name="bank") for i in first_tiles]
        for i in first_tiles:
            one_pass(open_banks[i], i, 0, 0)
        quantise_weights_half(ROUNDS, 0)
        quantise_weights_half(ROUNDS, 1)
        pair_factors()
        transpose_tokens(4, False)
        transpose_tokens(5, True)
        for i in first_tiles:
            one_pass(open_banks[i], i, 0, 1)
            collect(open_banks[i], i, 0)
        quantise_tokens(4)
        quantise_tokens(5)
        transpose_tokens(6, True)
        transpose_tokens(7, True)
        transpose_weights(1, (True, False))
        quantise_tokens(6)
        quantise_tokens(7)
        transpose_weights(1 + ROUNDS, (True, False))
        quantise_weights(1)
        quantise_weights(1 + ROUNDS)
        multiply(0, last_tiles)
        for tiles, j in ((first_tiles, 2), (last_tiles, 3)):
            transpose_weights(j, (False, False))
            transpose_weights(j + ROUNDS, (False, False))
            multiply(1, tiles[:2])
            quantise_weights(j)
            multiply(1, tiles[2:])
            quantise_weights(j + ROUNDS)
        for tiles in (first_tiles, last_tiles):
            multiply(2, tiles)
            multiply(3, tiles)
